import numpy as np
import ml_dtypes


def mxq(x, axis, fmt="e4m3"):
    dtype, down = {"e4m3": (ml_dtypes.float8_e4m3fn, 7), "e5m2": (ml_dtypes.float8_e5m2, 14)}[fmt]
    v = np.moveaxis(np.asarray(x, np.float32).astype(ml_dtypes.bfloat16).astype(np.float64), axis, -1)
    blocks = v.reshape(v.shape[:-1] + (-1, 32))
    amax = np.abs(blocks).max(-1, keepdims=True)
    byte = np.maximum(np.where(amax > 0, np.frexp(amax)[1] - 1 + 127, 0) - down, 1)
    scale = np.exp2(byte - 127.0)
    codes = (blocks / scale).astype(np.float32).astype(dtype).astype(np.float64)
    return np.moveaxis((codes * scale).reshape(v.shape), -1, axis)


WIDE = False


def mx_kscale(k):
    if not WIDE:
        return np.ones(k)
    levels = np.array([10, -10, 5, -5, 0])
    a = np.random.permutation(np.resize(levels, k // 512 * 4)).reshape(k // 512, 4)
    idx = np.arange(k)
    return np.exp2(a[idx // 512, idx % 128 // 32])


BF16 = ml_dtypes.bfloat16


def bf(x):
    return np.asarray(x, np.float32).astype(BF16)


def f64(x):
    return np.asarray(x).astype(np.float64)


E2M1 = np.array([0.0, 0.5, 1.0, 1.5, 2.0, 3.0, 4.0, 6.0, -0.0, -0.5, -1.0, -1.5, -2.0, -3.0, -4.0, -6.0])


def pack_weight(w, fmt):
    k, n = w.shape
    w = f64(bf(w)).reshape(k // 32, 32, n)
    amax = np.abs(w).max(1)
    if fmt == "e4m3":
        byte = np.frexp(amax)[1] - 1 + 127 - 7
    else:
        mant, ex = np.frexp(amax / 6.0)
        byte = np.where(mant > 0.5, ex, ex - 1) + 127
    byte = np.clip(np.where(amax > 0, byte, 1), 1, 254)
    scaled = (w * np.exp2(127.0 - byte)[:, None, :]).reshape(k, n).astype(np.float32)
    by_word = np.ascontiguousarray(scaled.reshape(k // 512, 128, 4, n).transpose(0, 1, 3, 2))
    if fmt == "e4m3":
        words = by_word.astype(ml_dtypes.float8_e4m3fn).view(np.uint8)
    else:
        c = by_word.astype(ml_dtypes.float4_e2m1fn).view(np.uint8) & 0xF
        words = c[..., 0::2] | (c[..., 1::2] << 4)
    return np.ascontiguousarray(words), np.ascontiguousarray(byte.astype(np.uint8).reshape(k // 512, 16, n))


def unpack_weight(words, scales, fmt):
    g, p, n, _ = words.shape
    if fmt == "e4m3":
        vals = np.ascontiguousarray(words).view(ml_dtypes.float8_e4m3fn).astype(np.float64)
    else:
        nib = np.empty((g, p, n, 4), np.uint8)
        nib[..., 0::2] = words & 0xF
        nib[..., 1::2] = words >> 4
        vals = E2M1[nib]
    vals = vals * np.repeat(np.exp2(scales.astype(np.float64) - 127.0), 8, axis=1)[..., None]
    return vals.transpose(0, 1, 3, 2).reshape(g * 512, n)


B, C, H, W, F, KH, KW = 32, 512, 4, 4, 4096, 3, 3
K = KH * KW * C
SPARSITY = 0.7
FMT = "e4m3"


def extract_patches(x, kh, kw):
    bb, s1, s2, cc = x.shape
    o1, o2 = s1 - kh + 1, s2 - kw + 1
    pats = np.stack([x[:, i:i + o1, j:j + o2, :] for i in range(kh) for j in range(kw)], axis=3)
    return pats.reshape(bb, o1, o2, kh * kw * cc)


def setup_inputs():
    s = mx_kscale(C)
    limit = np.sqrt(6.0 / (F + K))
    vals = np.random.uniform(-limit, limit, (F, K))
    mask = np.random.random((F, K)) >= SPARSITY
    mask[:, ::32] = True
    inputs = bf(np.random.standard_normal((B, C, H, W)) * s[None, :, None, None])
    kernel = vals * mask / np.tile(s, KH * KW)[None, :]
    words, scales = pack_weight(np.ascontiguousarray(kernel.T), FMT)
    return {"inputs": inputs, "kernel_words": words, "kernel_scales": scales}


def reference(inputs, kernel_words, kernel_scales):
    x = np.transpose(f64(inputs), (0, 3, 2, 1))
    p = extract_patches(x, KH, KW)
    p2 = np.ascontiguousarray(p.reshape(-1, K))
    wt = unpack_weight(kernel_words, kernel_scales, FMT)
    out = mxq(p2, 1, "e4m3") @ wt
    return out.reshape(p.shape[:3] + (F,)).transpose(0, 3, 1, 2)

@@ -1,0 +1,134 @@
+from contextlib import ExitStack
+
+import concourse.mybir as mybir
+from concourse.masks import make_identity
+
+BF16 = mybir.dt.bfloat16
+F32 = mybir.dt.float32
+I32 = mybir.dt.int32
+U32 = mybir.dt.uint32
+U8 = mybir.dt.uint8
+FP8X4 = mybir.dt.float8_e4m3fn_x4
+
+P = 128
+PACK = 4
+BATCH = 32
+IMAGE_SIDE = 4
+WINDOW_SIDE = 3
+OUT_SIDE = 2
+PLACES = OUT_SIDE * OUT_SIDE
+PASSES = WINDOW_SIDE * WINDOW_SIDE
+FILTERS = 4096
+BLOCK = 128
+QUAD = 4
+CHUNK = 1024
+CHUNKS = FILTERS // CHUNK
+BLOCKS_IN_CHUNK = CHUNK // BLOCK
+QUADS_IN_CHUNK = BLOCKS_IN_CHUNK // QUAD
+PSUM_BANKS = 8
+QUADRANT = 32
+SCALE_ROWS = 4
+PLANES_IN_TILE = 4
+PLANE_TILES = (PASSES + PLANES_IN_TILE - 1) // PLANES_IN_TILE
+
+FLOPS = 2 * BATCH * PLACES * PASSES * P * PACK * FILTERS
+
+
+def tile_sparseconv2d_w_kernel(tc, inputs, kernel_words, kernel_scales, out):
+    nc = tc.nc
+    with ExitStack() as stack:
+        keep = stack.enter_context(tc.tile_pool(name="keep", bufs=1))
+        turning = stack.enter_context(tc.tile_pool(name="turning", bufs=2))
+        leaving = stack.enter_context(tc.tile_pool(name="leaving", bufs=CHUNKS * QUADS_IN_CHUNK))
+        banks = stack.enter_context(tc.psum_pool(name="banks", bufs=PSUM_BANKS))
+
+        w_planes = keep.tile([P, PLANE_TILES, FILTERS], U8, align_bytes=64)
+        nc.vector.memset(w_planes[:].bitcast(I32), 0)
+        identity = keep.tile([P, P], F32)
+        make_identity(nc, identity[:])
+
+        image = keep.tile([P, BATCH * PACK, IMAGE_SIDE, IMAGE_SIDE], BF16)
+        nc.sync.dma_start(
+            out=image[:].rearrange("p (b t) h w -> p b (t h w)", t=PACK),
+            in_=inputs.rearrange("b (p t) h w -> p b (t h w)", t=PACK),
+        )
+
+        for plane_tile in range(PLANE_TILES):
+            first = plane_tile * PLANES_IN_TILE
+            planes = min(PLANES_IN_TILE, PASSES - first)
+            for quadrant in range(P // QUADRANT):
+                top = quadrant * QUADRANT
+                nc.sync.dma_start(
+                    out=w_planes[top : top + planes * SCALE_ROWS, plane_tile, :].bitcast(I32),
+                    in_=kernel_scales[
+                        first : first + planes, quadrant * SCALE_ROWS : (quadrant + 1) * SCALE_ROWS, :
+                    ].bitcast(I32),
+                )
+
+        w_words = []
+        for chunk in range(CHUNKS):
+            words = keep.tile([P, PASSES, CHUNK], I32, name="w_words%d" % chunk, align_bytes=64)
+            for g in range(PASSES):
+                all_filters = kernel_words[g].rearrange("p n t -> p (n t)")
+                nc.sync.dma_start(
+                    out=words[:, g, :],
+                    in_=all_filters[:, chunk * CHUNK * PACK : (chunk + 1) * CHUNK * PACK].bitcast(I32),
+                )
+            w_words.append(words)
+
+        patches = keep.tile([P, PASSES, P * PACK], BF16, align_bytes=64)
+        p_words = keep.tile([P, PASSES, P], U32, align_bytes=64)
+        p_planes = keep.tile([P, PASSES, P], U8, align_bytes=64)
+        for g in range(PASSES):
+            i, j = divmod(g, WINDOW_SIDE)
+            nc.vector.tensor_copy(
+                out=patches[:, g, :].rearrange("p (a d q) -> p a d q", a=OUT_SIDE, d=OUT_SIDE),
+                in_=image[:, :, j : j + OUT_SIDE, i : i + OUT_SIDE].rearrange("p q d a -> p a d q"),
+            )
+        for g in range(PASSES):
+            nc.vector.quantize_mx(
+                out=p_words[:, g, :].bitcast(FP8X4),
+                scales=p_planes[:, g, :],
+                in_=patches[:, g, :],
+            )
+
+        out_rows = out.rearrange("b (q h f) a d -> q b h (f a d)", h=QUAD, f=BLOCK)
+        for chunk in range(CHUNKS):
+            sums = [
+                banks.tile([P, P], F32, name="sums%d" % block, tag="bank")
+                for block in range(BLOCKS_IN_CHUNK)
+            ]
+            for g in range(PASSES):
+                plane_top = (g % PLANES_IN_TILE) * SCALE_ROWS
+                for block in range(BLOCKS_IN_CHUNK):
+                    in_chunk = slice(block * BLOCK, (block + 1) * BLOCK)
+                    in_all = slice(chunk * CHUNK + block * BLOCK, chunk * CHUNK + (block + 1) * BLOCK)
+                    nc.tensor.matmul_mx(
+                        out=sums[block][:],
+                        lhsT=w_words[chunk][:, g, in_chunk].bitcast(FP8X4),
+                        lhsT_scale=w_planes[plane_top:P, g // PLANES_IN_TILE, in_all],
+                        rhs=p_words[:, g, :].bitcast(FP8X4),
+                        rhs_scale=p_planes[:, g, :],
+                        start=(g == 0),
+                        stop=(g == PASSES - 1),
+                    )
+
+            for quad in range(QUADS_IN_CHUNK):
+                by_filter = turning.tile([P, BATCH, QUAD, PLACES], F32, align_bytes=64)
+                for h in range(QUAD):
+                    copy = nc.vector.tensor_copy if h < QUAD // 2 else nc.scalar.copy
+                    copy(
+                        out=by_filter[:, :, h, :],
+                        in_=sums[quad * QUAD + h][:].rearrange("p (s b) -> p b s", s=PLACES),
+                    )
+                by_image = banks.tile([P, PLACES, BLOCK], F32, tag="bank")
+                columns = by_filter[:].rearrange("p b h s -> p (b h) s")
+                for s in range(PLACES):
+                    nc.tensor.transpose(by_image[:, s, :], columns[:, :, s], identity[:])
+                row = leaving.tile([P, BLOCK, PLACES], F32)
+                copy = nc.vector.tensor_copy if quad % 2 == 0 else nc.scalar.copy
+                copy(out=row[:], in_=by_image[:].rearrange("p s f -> p f s"))
+                nc.sync.dma_start(
+                    out=out_rows[chunk * QUADS_IN_CHUNK + quad],
+                    in_=row[:].rearrange("p f s -> p (f s)"),
+                )

@@ -58,11 +58,11 @@ def tile_sparseconv2d_w_kernel(tc, inputs, kernel_words, kernel_scales, out):
             planes = min(PLANES_IN_TILE, PASSES - first)
             for quadrant in range(P // QUADRANT):
                 top = quadrant * QUADRANT
-                nc.sync.dma_start(
-                    out=w_planes[top : top + planes * SCALE_ROWS, plane_tile, :].bitcast(I32),
+                nc.gpsimd.dma_start(
+                    out=w_planes[top : top + planes * SCALE_ROWS, plane_tile, :].bitcast(F32),
                     in_=kernel_scales[
                         first : first + planes, quadrant * SCALE_ROWS : (quadrant + 1) * SCALE_ROWS, :
-                    ].bitcast(I32),
+                    ].bitcast(F32),
                 )
 
         w_words = []

@@ -27,6 +27,8 @@ BLOCKS_IN_CHUNK = CHUNK // BLOCK
 QUADS_IN_CHUNK = BLOCKS_IN_CHUNK // QUAD
 PSUM_BANKS = 8
 QUADRANT = 32
+PIXELS = IMAGE_SIDE * IMAGE_SIDE
+HALVES = 2
 SCALE_ROWS = 4
 PLANES_IN_TILE = 4
 PLANE_TILES = (PASSES + PLANES_IN_TILE - 1) // PLANES_IN_TILE
@@ -47,11 +49,12 @@ def tile_sparseconv2d_w_kernel(tc, inputs, kernel_words, kernel_scales, out):
         identity = keep.tile([P, P], F32)
         make_identity(nc, identity[:])
 
-        image = keep.tile([P, BATCH * PACK, IMAGE_SIDE, IMAGE_SIDE], BF16)
-        nc.sync.dma_start(
-            out=image[:].rearrange("p (b t) h w -> p b (t h w)", t=PACK),
-            in_=inputs.rearrange("b (p t) h w -> p b (t h w)", t=PACK),
-        )
+        by_batch = keep.tile([P, QUADRANT * PACK * PIXELS], BF16, align_bytes=64)
+        for q in range(P // QUADRANT):
+            nc.sync.dma_start(
+                out=by_batch[q * QUADRANT : (q + 1) * QUADRANT, :],
+                in_=inputs[:, q * P : (q + 1) * P, :, :].rearrange("b c h w -> b (c h w)"),
+            )
 
         for plane_tile in range(PLANE_TILES):
             first = plane_tile * PLANES_IN_TILE
@@ -76,20 +79,31 @@ def tile_sparseconv2d_w_kernel(tc, inputs, kernel_words, kernel_scales, out):
                 )
             w_words.append(words)
 
-        patches = keep.tile([P, PASSES, P * PACK], BF16, align_bytes=64)
-        p_words = keep.tile([P, PASSES, P], U32, align_bytes=64)
-        p_planes = keep.tile([P, PASSES, P], U8, align_bytes=64)
-        for g in range(PASSES):
-            i, j = divmod(g, WINDOW_SIDE)
+        gathered = keep.tile([P, HALVES, PIXELS, QUADRANT, HALVES], BF16, align_bytes=64)
+        spread = by_batch[:].rearrange(
+            "p (l u v x) -> p u x l v", l=QUADRANT, u=HALVES, v=HALVES, x=PIXELS
+        )
+        for u in range(HALVES):
+            nc.vector.tensor_copy(out=gathered[:, u, :, :, :], in_=spread[:, u, :, :, :])
+        turned = keep.tile([P, HALVES * PIXELS * BATCH], F32, align_bytes=64)
+        nc.vector.transpose(
+            out=turned[:], in_=gathered[:].rearrange("p u x l v -> p (u x l v)").bitcast(F32)
+        )
+        by_pixel = turned[:].rearrange("p (u h w b) -> p u h w b", u=HALVES, h=IMAGE_SIDE, w=IMAGE_SIDE)
+        strip = IMAGE_SIDE * OUT_SIDE * BATCH
+        patches = keep.tile([P, WINDOW_SIDE, strip * PACK], BF16, align_bytes=64)
+        p_words = keep.tile([P, WINDOW_SIDE, strip], U32, align_bytes=64)
+        p_planes = keep.tile([P, WINDOW_SIDE, strip], U8, align_bytes=64)
+        for i in range(WINDOW_SIDE):
             nc.vector.tensor_copy(
-                out=patches[:, g, :].rearrange("p (a d q) -> p a d q", a=OUT_SIDE, d=OUT_SIDE),
-                in_=image[:, :, j : j + OUT_SIDE, i : i + OUT_SIDE].rearrange("p q d a -> p a d q"),
+                out=patches[:, i, :].bitcast(F32).rearrange("p (h n u) -> p h n u", h=IMAGE_SIDE, u=HALVES),
+                in_=by_pixel[:, :, :, i : i + OUT_SIDE, :].rearrange("p u h a b -> p h (a b) u"),
             )
-        for g in range(PASSES):
+        for i in range(WINDOW_SIDE):
             nc.vector.quantize_mx(
-                out=p_words[:, g, :].bitcast(FP8X4),
-                scales=p_planes[:, g, :],
-                in_=patches[:, g, :],
+                out=p_words[:, i, :].bitcast(FP8X4),
+                scales=p_planes[:, i, :],
+                in_=patches[:, i, :],
             )
 
         out_rows = out.rearrange("b (q h f) a d -> q b h (f a d)", h=QUAD, f=BLOCK)
@@ -99,6 +113,8 @@ def tile_sparseconv2d_w_kernel(tc, inputs, kernel_words, kernel_scales, out):
                 for block in range(BLOCKS_IN_CHUNK)
             ]
             for g in range(PASSES):
+                i, j = divmod(g, WINDOW_SIDE)
+                window = slice(j * OUT_SIDE * BATCH, (j + OUT_SIDE) * OUT_SIDE * BATCH)
                 plane_top = (g % PLANES_IN_TILE) * SCALE_ROWS
                 for block in range(BLOCKS_IN_CHUNK):
                     in_chunk = slice(block * BLOCK, (block + 1) * BLOCK)
@@ -107,8 +123,8 @@ def tile_sparseconv2d_w_kernel(tc, inputs, kernel_words, kernel_scales, out):
                         out=sums[block][:],
                         lhsT=w_words[chunk][:, g, in_chunk].bitcast(FP8X4),
                         lhsT_scale=w_planes[plane_top:P, g // PLANES_IN_TILE, in_all],
-                        rhs=p_words[:, g, :].bitcast(FP8X4),
-                        rhs_scale=p_planes[:, g, :],
+                        rhs=p_words[:, i, window].bitcast(FP8X4),
+                        rhs_scale=p_planes[:, i, window],
                         start=(g == 0),
                         stop=(g == PASSES - 1),
                     )
@@ -124,7 +140,8 @@ def tile_sparseconv2d_w_kernel(tc, inputs, kernel_words, kernel_scales, out):
                 by_image = banks.tile([P, PLACES, BLOCK], F32, tag="bank")
                 columns = by_filter[:].rearrange("p b h s -> p (b h) s")
                 for s in range(PLACES):
-                    nc.tensor.transpose(by_image[:, s, :], columns[:, :, s], identity[:])
+                    d, a = divmod(s, OUT_SIDE)
+                    nc.tensor.transpose(by_image[:, a * OUT_SIDE + d, :], columns[:, :, s], identity[:])
                 row = leaving.tile([P, BLOCK, PLACES], F32)
                 copy = nc.vector.tensor_copy if quad % 2 == 0 else nc.scalar.copy
                 copy(out=row[:], in_=by_image[:].rearrange("p s f -> p f s"))

@@ -26,6 +26,7 @@ CHUNKS = FILTERS // CHUNK
 BLOCKS_IN_CHUNK = CHUNK // BLOCK
 QUADS_IN_CHUNK = BLOCKS_IN_CHUNK // QUAD
 PSUM_BANKS = 8
+DMA_ALIGN = 4096
 QUADRANT = 32
 PIXELS = IMAGE_SIDE * IMAGE_SIDE
 HALVES = 2
@@ -44,12 +45,12 @@ def tile_sparseconv2d_w_kernel(tc, inputs, kernel_words, kernel_scales, out):
         leaving = stack.enter_context(tc.tile_pool(name="leaving", bufs=CHUNKS * QUADS_IN_CHUNK))
         banks = stack.enter_context(tc.psum_pool(name="banks", bufs=PSUM_BANKS))
 
-        w_planes = keep.tile([P, PLANE_TILES, FILTERS], U8, align_bytes=64)
+        w_planes = keep.tile([P, PLANE_TILES, FILTERS], U8, align_bytes=DMA_ALIGN)
         nc.vector.memset(w_planes[:].bitcast(I32), 0)
         identity = keep.tile([P, P], F32)
         make_identity(nc, identity[:])
 
-        by_batch = keep.tile([P, QUADRANT * PACK * PIXELS], BF16, align_bytes=64)
+        by_batch = keep.tile([P, QUADRANT * PACK * PIXELS], BF16, align_bytes=DMA_ALIGN)
         for q in range(P // QUADRANT):
             nc.sync.dma_start(
                 out=by_batch[q * QUADRANT : (q + 1) * QUADRANT, :],
@@ -70,7 +71,7 @@ def tile_sparseconv2d_w_kernel(tc, inputs, kernel_words, kernel_scales, out):
 
         w_words = []
         for chunk in range(CHUNKS):
-            words = keep.tile([P, PASSES, CHUNK], I32, name="w_words%d" % chunk, align_bytes=64)
+            words = keep.tile([P, PASSES, CHUNK], I32, name="w_words%d" % chunk, align_bytes=DMA_ALIGN)
             for g in range(PASSES):
                 all_filters = kernel_words[g].rearrange("p n t -> p (n t)")
                 nc.sync.dma_start(
@@ -142,7 +143,7 @@ def tile_sparseconv2d_w_kernel(tc, inputs, kernel_words, kernel_scales, out):
                 for s in range(PLACES):
                     d, a = divmod(s, OUT_SIDE)
                     nc.tensor.transpose(by_image[:, a * OUT_SIDE + d, :], columns[:, :, s], identity[:])
-                row = leaving.tile([P, BLOCK, PLACES], F32)
+                row = leaving.tile([P, BLOCK, PLACES], F32, align_bytes=BLOCK * PLACES * 4)
                 copy = nc.vector.tensor_copy if quad % 2 == 0 else nc.scalar.copy
                 copy(out=row[:], in_=by_image[:].rearrange("p s f -> p f s"))
                 nc.sync.dma_start(

@@ -46,13 +46,15 @@ def tile_sparseconv2d_w_kernel(tc, inputs, kernel_words, kernel_scales, out):
         banks = stack.enter_context(tc.psum_pool(name="banks", bufs=PSUM_BANKS))
 
         w_planes = keep.tile([P, PLANE_TILES, FILTERS], U8, align_bytes=DMA_ALIGN)
-        nc.vector.memset(w_planes[:].bitcast(I32), 0)
+        for plane_tile in range(PLANE_TILES):
+            nc.vector.memset(w_planes[:, plane_tile, :].bitcast(I32), 0)
         identity = keep.tile([P, P], F32)
         make_identity(nc, identity[:])
 
         by_batch = keep.tile([P, QUADRANT * PACK * PIXELS], BF16, align_bytes=DMA_ALIGN)
         for q in range(P // QUADRANT):
-            nc.sync.dma_start(
+            queue = nc.sync if q < P // QUADRANT // HALVES else nc.scalar
+            queue.dma_start(
                 out=by_batch[q * QUADRANT : (q + 1) * QUADRANT, :],
                 in_=inputs[:, q * P : (q + 1) * P, :, :].rearrange("b c h w -> b (c h w)"),
             )
@@ -80,32 +82,60 @@ def tile_sparseconv2d_w_kernel(tc, inputs, kernel_words, kernel_scales, out):
                 )
             w_words.append(words)
 
-        gathered = keep.tile([P, HALVES, PIXELS, QUADRANT, HALVES], BF16, align_bytes=64)
+        gathered = keep.tile([P, HALVES, HALVES, IMAGE_SIDE, HALVES, QUADRANT, HALVES], BF16, align_bytes=64)
         spread = by_batch[:].rearrange(
-            "p (l u v x) -> p u x l v", l=QUADRANT, u=HALVES, v=HALVES, x=PIXELS
+            "p (l u v h c e) -> p c u e h l v",
+            l=QUADRANT, u=HALVES, v=HALVES, h=IMAGE_SIDE, c=HALVES, e=HALVES,
         )
-        for u in range(HALVES):
-            nc.vector.tensor_copy(out=gathered[:, u, :, :, :], in_=spread[:, u, :, :, :])
-        turned = keep.tile([P, HALVES * PIXELS * BATCH], F32, align_bytes=64)
-        nc.vector.transpose(
-            out=turned[:], in_=gathered[:].rearrange("p u x l v -> p (u x l v)").bitcast(F32)
-        )
-        by_pixel = turned[:].rearrange("p (u h w b) -> p u h w b", u=HALVES, h=IMAGE_SIDE, w=IMAGE_SIDE)
+        turned = keep.tile([P, HALVES, HALVES * IMAGE_SIDE * HALVES * BATCH], F32, align_bytes=64)
+
+        def gather(c):
+            for u in range(HALVES):
+                copy = nc.vector.tensor_copy if u == 0 else nc.scalar.copy
+                for e in range(HALVES):
+                    copy(out=gathered[:, c, u, :, e, :, :], in_=spread[:, c, u, e, :, :, :])
+
+        def turn(c):
+            nc.vector.transpose(
+                out=turned[:, c, :],
+                in_=gathered[:, c, :, :, :, :, :].rearrange("p u h e l v -> p (u h e l v)").bitcast(F32),
+            )
+
         strip = IMAGE_SIDE * OUT_SIDE * BATCH
         patches = keep.tile([P, WINDOW_SIDE, strip * PACK], BF16, align_bytes=64)
         p_words = keep.tile([P, WINDOW_SIDE, strip], U32, align_bytes=64)
         p_planes = keep.tile([P, WINDOW_SIDE, strip], U8, align_bytes=64)
-        for i in range(WINDOW_SIDE):
-            nc.vector.tensor_copy(
-                out=patches[:, i, :].bitcast(F32).rearrange("p (h n u) -> p h n u", h=IMAGE_SIDE, u=HALVES),
-                in_=by_pixel[:, :, :, i : i + OUT_SIDE, :].rearrange("p u h a b -> p h (a b) u"),
+
+        def interleave(copy, i):
+            by_column = patches[:, i, :].bitcast(F32).rearrange(
+                "p (h a b u) -> p h a b u", h=IMAGE_SIDE, a=OUT_SIDE, u=HALVES
             )
-        for i in range(WINDOW_SIDE):
+            if i % HALVES == 0:
+                copy(
+                    out=patches[:, i, :].bitcast(F32).rearrange("p (h n u) -> p h n u", h=IMAGE_SIDE, u=HALVES),
+                    in_=turned[:, i // HALVES, :].rearrange("p (u h n) -> p h n u", u=HALVES, h=IMAGE_SIDE),
+                )
+            else:
+                for a in range(OUT_SIDE):
+                    c, e = divmod(i + a, HALVES)
+                    by_pixel = turned[:, c, :].rearrange("p (u h e b) -> p e h b u", u=HALVES, h=IMAGE_SIDE, e=HALVES)
+                    copy(out=by_column[:, :, a, :, :], in_=by_pixel[:, e, :, :, :])
+
+        def quantize(i):
             nc.vector.quantize_mx(
-                out=p_words[:, i, :].bitcast(FP8X4),
-                scales=p_planes[:, i, :],
-                in_=patches[:, i, :],
+                out=p_words[:, i, :].bitcast(FP8X4), scales=p_planes[:, i, :], in_=patches[:, i, :]
             )
+
+        gather(0)
+        turn(0)
+        interleave(nc.vector.tensor_copy, 0)
+        gather(1)
+        quantize(0)
+        turn(1)
+        interleave(nc.vector.tensor_copy, 1)
+        interleave(nc.scalar.copy, 2)
+        quantize(1)
+        quantize(2)
 
         out_rows = out.rearrange("b (q h f) a d -> q b h (f a d)", h=QUAD, f=BLOCK)
         for chunk in range(CHUNKS):

from contextlib import ExitStack

import concourse.mybir as mybir
from concourse.masks import make_identity

BF16 = mybir.dt.bfloat16
F32 = mybir.dt.float32
I32 = mybir.dt.int32
U32 = mybir.dt.uint32
U8 = mybir.dt.uint8
FP8X4 = mybir.dt.float8_e4m3fn_x4

P = 128
PACK = 4
BATCH = 32
IMAGE_SIDE = 4
WINDOW_SIDE = 3
OUT_SIDE = 2
PLACES = OUT_SIDE * OUT_SIDE
PASSES = WINDOW_SIDE * WINDOW_SIDE
FILTERS = 4096
BLOCK = 128
QUAD = 4
CHUNK = 1024
CHUNKS = FILTERS // CHUNK
BLOCKS_IN_CHUNK = CHUNK // BLOCK
QUADS_IN_CHUNK = BLOCKS_IN_CHUNK // QUAD
PSUM_BANKS = 8
DMA_ALIGN = 4096
QUADRANT = 32
PIXELS = IMAGE_SIDE * IMAGE_SIDE
HALVES = 2
SCALE_ROWS = 4
PLANES_IN_TILE = 4
PLANE_TILES = (PASSES + PLANES_IN_TILE - 1) // PLANES_IN_TILE

FLOPS = 2 * BATCH * PLACES * PASSES * P * PACK * FILTERS


def tile_sparseconv2d_w_kernel(tc, inputs, kernel_words, kernel_scales, out):
    nc = tc.nc
    with ExitStack() as stack:
        keep = stack.enter_context(tc.tile_pool(name="keep", bufs=1))
        turning = stack.enter_context(tc.tile_pool(name="turning", bufs=2))
        leaving = stack.enter_context(tc.tile_pool(name="leaving", bufs=CHUNKS * QUADS_IN_CHUNK))
        banks = stack.enter_context(tc.psum_pool(name="banks", bufs=PSUM_BANKS))

        w_planes = keep.tile([P, PLANE_TILES, FILTERS], U8, align_bytes=DMA_ALIGN)
        for plane_tile in range(PLANE_TILES):
            nc.vector.memset(w_planes[:, plane_tile, :].bitcast(I32), 0)
        identity = keep.tile([P, P], F32)
        make_identity(nc, identity[:])

        by_batch = keep.tile([P, QUADRANT * PACK * PIXELS], BF16, align_bytes=DMA_ALIGN)
        for q in range(P // QUADRANT):
            queue = nc.sync if q < P // QUADRANT // HALVES else nc.scalar
            queue.dma_start(
                out=by_batch[q * QUADRANT : (q + 1) * QUADRANT, :],
                in_=inputs[:, q * P : (q + 1) * P, :, :].rearrange("b c h w -> b (c h w)"),
            )

        for plane_tile in range(PLANE_TILES):
            first = plane_tile * PLANES_IN_TILE
            planes = min(PLANES_IN_TILE, PASSES - first)
            for quadrant in range(P // QUADRANT):
                top = quadrant * QUADRANT
                nc.gpsimd.dma_start(
                    out=w_planes[top : top + planes * SCALE_ROWS, plane_tile, :].bitcast(F32),
                    in_=kernel_scales[
                        first : first + planes, quadrant * SCALE_ROWS : (quadrant + 1) * SCALE_ROWS, :
                    ].bitcast(F32),
                )

        w_words = []
        for chunk in range(CHUNKS):
            words = keep.tile([P, PASSES, CHUNK], I32, name="w_words%d" % chunk, align_bytes=DMA_ALIGN)
            for g in range(PASSES):
                all_filters = kernel_words[g].rearrange("p n t -> p (n t)")
                nc.sync.dma_start(
                    out=words[:, g, :],
                    in_=all_filters[:, chunk * CHUNK * PACK : (chunk + 1) * CHUNK * PACK].bitcast(I32),
                )
            w_words.append(words)

        gathered = keep.tile([P, HALVES, HALVES, IMAGE_SIDE, HALVES, QUADRANT, HALVES], BF16, align_bytes=64)
        spread = by_batch[:].rearrange(
            "p (l u v h c e) -> p c u e h l v",
            l=QUADRANT, u=HALVES, v=HALVES, h=IMAGE_SIDE, c=HALVES, e=HALVES,
        )
        turned = keep.tile([P, HALVES, HALVES * IMAGE_SIDE * HALVES * BATCH], F32, align_bytes=64)

        def gather(c):
            for u in range(HALVES):
                copy = nc.vector.tensor_copy if u == 0 else nc.scalar.copy
                for e in range(HALVES):
                    copy(out=gathered[:, c, u, :, e, :, :], in_=spread[:, c, u, e, :, :, :])

        def turn(c):
            nc.vector.transpose(
                out=turned[:, c, :],
                in_=gathered[:, c, :, :, :, :, :].rearrange("p u h e l v -> p (u h e l v)").bitcast(F32),
            )

        strip = IMAGE_SIDE * OUT_SIDE * BATCH
        patches = keep.tile([P, WINDOW_SIDE, strip * PACK], BF16, align_bytes=64)
        p_words = keep.tile([P, WINDOW_SIDE, strip], U32, align_bytes=64)
        p_planes = keep.tile([P, WINDOW_SIDE, strip], U8, align_bytes=64)

        def interleave(copy, i):
            by_column = patches[:, i, :].bitcast(F32).rearrange(
                "p (h a b u) -> p h a b u", h=IMAGE_SIDE, a=OUT_SIDE, u=HALVES
            )
            if i % HALVES == 0:
                copy(
                    out=patches[:, i, :].bitcast(F32).rearrange("p (h n u) -> p h n u", h=IMAGE_SIDE, u=HALVES),
                    in_=turned[:, i // HALVES, :].rearrange("p (u h n) -> p h n u", u=HALVES, h=IMAGE_SIDE),
                )
            else:
                for a in range(OUT_SIDE):
                    c, e = divmod(i + a, HALVES)
                    by_pixel = turned[:, c, :].rearrange("p (u h e b) -> p e h b u", u=HALVES, h=IMAGE_SIDE, e=HALVES)
                    copy(out=by_column[:, :, a, :, :], in_=by_pixel[:, e, :, :, :])

        def quantize(i):
            nc.vector.quantize_mx(
                out=p_words[:, i, :].bitcast(FP8X4), scales=p_planes[:, i, :], in_=patches[:, i, :]
            )

        gather(0)
        turn(0)
        interleave(nc.vector.tensor_copy, 0)
        gather(1)
        quantize(0)
        turn(1)
        interleave(nc.vector.tensor_copy, 1)
        interleave(nc.scalar.copy, 2)
        quantize(1)
        quantize(2)

        out_rows = out.rearrange("b (q h f) a d -> q b h (f a d)", h=QUAD, f=BLOCK)
        for chunk in range(CHUNKS):
            sums = [
                banks.tile([P, P], F32, name="sums%d" % block, tag="bank")
                for block in range(BLOCKS_IN_CHUNK)
            ]
            for g in range(PASSES):
                i, j = divmod(g, WINDOW_SIDE)
                window = slice(j * OUT_SIDE * BATCH, (j + OUT_SIDE) * OUT_SIDE * BATCH)
                plane_top = (g % PLANES_IN_TILE) * SCALE_ROWS
                for block in range(BLOCKS_IN_CHUNK):
                    in_chunk = slice(block * BLOCK, (block + 1) * BLOCK)
                    in_all = slice(chunk * CHUNK + block * BLOCK, chunk * CHUNK + (block + 1) * BLOCK)
                    nc.tensor.matmul_mx(
                        out=sums[block][:],
                        lhsT=w_words[chunk][:, g, in_chunk].bitcast(FP8X4),
                        lhsT_scale=w_planes[plane_top:P, g // PLANES_IN_TILE, in_all],
                        rhs=p_words[:, i, window].bitcast(FP8X4),
                        rhs_scale=p_planes[:, i, window],
                        start=(g == 0),
                        stop=(g == PASSES - 1),
                    )

            for quad in range(QUADS_IN_CHUNK):
                by_filter = turning.tile([P, BATCH, QUAD, PLACES], F32, align_bytes=64)
                for h in range(QUAD):
                    copy = nc.vector.tensor_copy if h < QUAD // 2 else nc.scalar.copy
                    copy(
                        out=by_filter[:, :, h, :],
                        in_=sums[quad * QUAD + h][:].rearrange("p (s b) -> p b s", s=PLACES),
                    )
                by_image = banks.tile([P, PLACES, BLOCK], F32, tag="bank")
                columns = by_filter[:].rearrange("p b h s -> p (b h) s")
                for s in range(PLACES):
                    d, a = divmod(s, OUT_SIDE)
                    nc.tensor.transpose(by_image[:, a * OUT_SIDE + d, :], columns[:, :, s], identity[:])
                row = leaving.tile([P, BLOCK, PLACES], F32, align_bytes=BLOCK * PLACES * 4)
                copy = nc.vector.tensor_copy if quad % 2 == 0 else nc.scalar.copy
                copy(out=row[:], in_=by_image[:].rearrange("p s f -> p f s"))
                nc.sync.dma_start(
                    out=out_rows[chunk * QUADS_IN_CHUNK + quad],
                    in_=row[:].rearrange("p f s -> p (f s)"),
                )
